import numpy as np
import ml_dtypes


def mxq(x, axis, fmt="e4m3"):
    dtype, down = {"e4m3": (ml_dtypes.float8_e4m3fn, 7), "e5m2": (ml_dtypes.float8_e5m2, 14)}[fmt]
    v = np.moveaxis(np.asarray(x, np.float32).astype(ml_dtypes.bfloat16).astype(np.float64), axis, -1)
    blocks = v.reshape(v.shape[:-1] + (-1, 32))
    amax = np.abs(blocks).max(-1, keepdims=True)
    byte = np.maximum(np.where(amax > 0, np.frexp(amax)[1] - 1 + 127, 0) - down, 1)
    scale = np.exp2(byte - 127.0)
    codes = (blocks / scale).astype(np.float32).astype(dtype).astype(np.float64)
    return np.moveaxis((codes * scale).reshape(v.shape), -1, axis)


WIDE = False


def mx_kscale(k):
    if not WIDE:
        return np.ones(k)
    levels = np.array([10, -10, 5, -5, 0])
    if k % 512:
        return np.exp2(np.random.permutation(np.resize(levels, k // 32))).repeat(32)
    a = np.empty((k // 512, 16))
    for p in range(k // 512):
        a[p, :8] = np.random.permutation(np.resize(levels, 8))
        for g in range(8):
            far = levels[np.abs(levels - a[p, g]) >= 10]
            a[p, g + 8] = far[np.random.randint(len(far))]
    return np.exp2(a.ravel()).repeat(32)


BF16 = ml_dtypes.bfloat16


def bf(x):
    return np.asarray(x, np.float32).astype(BF16)


def f64(x):
    return np.asarray(x).astype(np.float64)


E2M1 = np.array([0.0, 0.5, 1.0, 1.5, 2.0, 3.0, 4.0, 6.0, -0.0, -0.5, -1.0, -1.5, -2.0, -3.0, -4.0, -6.0])


def pack_weight(w, fmt):
    k, n = w.shape
    w = f64(bf(w)).reshape(k // 32, 32, n)
    amax = np.abs(w).max(1)
    if fmt == "e4m3":
        byte = np.frexp(amax)[1] - 1 + 127 - 7
    else:
        mant, ex = np.frexp(amax / 6.0)
        byte = np.where(mant > 0.5, ex, ex - 1) + 127
    byte = np.clip(np.where(amax > 0, byte, 1), 1, 254)
    scaled = (w * np.exp2(127.0 - byte)[:, None, :]).reshape(k, n).astype(np.float32)
    by_word = np.ascontiguousarray(scaled.reshape(k // 512, 128, 4, n).transpose(0, 1, 3, 2))
    if fmt == "e4m3":
        words = by_word.astype(ml_dtypes.float8_e4m3fn).view(np.uint8)
    else:
        c = by_word.astype(ml_dtypes.float4_e2m1fn).view(np.uint8) & 0xF
        words = c[..., 0::2] | (c[..., 1::2] << 4)
    return np.ascontiguousarray(words), np.ascontiguousarray(byte.astype(np.uint8).reshape(k // 512, 16, n))


def unpack_weight(words, scales, fmt):
    g, p, n, _ = words.shape
    if fmt == "e4m3":
        vals = np.ascontiguousarray(words).view(ml_dtypes.float8_e4m3fn).astype(np.float64)
    else:
        nib = np.empty((g, p, n, 4), np.uint8)
        nib[..., 0::2] = words & 0xF
        nib[..., 1::2] = words >> 4
        vals = E2M1[nib]
    vals = vals * np.repeat(np.exp2(scales.astype(np.float64) - 127.0), 8, axis=1)[..., None]
    return vals.transpose(0, 1, 3, 2).reshape(g * 512, n)


B, C, HH, WW, M, L, G, HID = 4, 1536, 32, 32, 128, 512, 256, 512
N = HH * WW
ITERS = 3
DUST = 1.0


def lse(a, axis):
    top = a.max(axis=axis, keepdims=True)
    return np.log(np.exp(a - top).sum(axis=axis)) + np.squeeze(top, axis=axis)


def draw0():
    s, t = mx_kscale(C), mx_kscale(HID)
    x = bf(np.random.standard_normal((B, C, HH, WW)) * s[None, :, None, None])
    Ws1 = np.random.standard_normal((HID, C)) / np.sqrt(C) / s[None, :] * t[:, None]
    Ws1_words, Ws1_scales = pack_weight(np.ascontiguousarray(Ws1.T), "e4m3")
    bs1 = bf(np.random.standard_normal(HID) * 0.3 * t)
    Ws2 = np.random.standard_normal((M, HID)) * 2.0 / np.sqrt(HID) / t[None, :]
    Ws2_words, Ws2_scales = pack_weight(np.ascontiguousarray(Ws2.T), "e4m3")
    return {
        "x": x,
        "Ws1_words": Ws1_words,
        "Ws1_scales": Ws1_scales,
        "bs1": bs1,
        "Ws2_words": Ws2_words,
        "Ws2_scales": Ws2_scales,
    }


def core(x, Ws1_words, Ws1_scales, bs1, Ws2_words, Ws2_scales):
    xf = f64(x).reshape(B, C, N)
    hs = np.maximum((unpack_weight(Ws1_words, Ws1_scales, "e4m3").T @ mxq(xf, 1, "e4m3")) + f64(bs1)[None, :, None], 0.0)
    p = unpack_weight(Ws2_words, Ws2_scales, "e4m3").T @ mxq(hs, 1, "e4m3")
    norm = -np.log(M + N)
    log_mu = np.concatenate([np.full(M, norm), np.full(1, np.log(N) + norm)])
    log_nu = np.full(N, norm)
    Z = np.concatenate([p, np.full((B, 1, N), DUST)], axis=1)
    u = np.zeros((B, M + 1))
    v = np.zeros((B, N))
    for _ in range(ITERS):
        u = log_mu[None] - lse(Z + v[:, None, :], 2)
        v = log_nu[None] - lse(Z + u[:, :, None], 1)
    return np.exp(Z + u[:, :, None] + v[:, None, :] - norm)[:, :-1, :]


def e4m3fn_bytes(y):
    return np.clip(np.asarray(y, np.float64), -448.0, 448.0).astype(np.float32).astype(ml_dtypes.float8_e4m3fn).view(np.uint8)


def e4m3fn_values(b):
    return np.asarray(b, np.uint8).view(ml_dtypes.float8_e4m3fn).astype(np.float64)


def setup_inputs():
    d = draw0()
    x0 = np.asarray(d['x']).astype(np.float64)
    s = (np.max(np.abs(x0), axis=(0, 2, 3), keepdims=True) / 448.0).astype(np.float32)
    out = {}
    for k, v in d.items():
        if k == 'x':
            out['x_bytes'] = e4m3fn_bytes(x0 / s.astype(np.float64))
            out['x_scale'] = s
        else:
            out[k] = v
    return out


def reference(x_bytes, x_scale, Ws1_words, Ws1_scales, bs1, Ws2_words, Ws2_scales):
    return core(e4m3fn_values(x_bytes) * x_scale.astype(np.float64), Ws1_words, Ws1_scales, bs1, Ws2_words, Ws2_scales)

from contextlib import ExitStack

import concourse.mybir as mybir
from concourse.masks import make_identity

F32 = mybir.dt.float32
BF16 = mybir.dt.bfloat16
I32 = mybir.dt.int32
U32 = mybir.dt.uint32
U8 = mybir.dt.uint8
F8 = mybir.dt.float8_e4m3fn
F8X4 = mybir.dt.float8_e4m3fn_x4
ALU = mybir.AluOpType
ACT = mybir.ActivationFunctionType
AX = mybir.AxisListType

P = 128
T = 4
IMAGES = 4
CHANNELS = 1536
PASSES = 3
PIXELS = 1024
HALF = 512
HALVES = 2
HIDDEN = 512
CLUSTERS = 128
CHUNKS = PIXELS // P
ROUNDS = 3

FLOPS = 2 * IMAGES * PIXELS * (CHANNELS * HIDDEN + HIDDEN * CLUSTERS)


def tile_salad_pa_w8_kernel(tc, x_bytes, x_scale, Ws1_words, Ws1_scales, bs1, Ws2_words, Ws2_scales, out):
    nc = tc.nc
    with ExitStack() as ctx:
        keep = ctx.enter_context(tc.tile_pool(name="keep", bufs=1))
        work = ctx.enter_context(tc.tile_pool(name="work", bufs=2))
        psum_acc = ctx.enter_context(tc.psum_pool(name="psum_acc", bufs=3))
        psum_p = ctx.enter_context(tc.psum_pool(name="psum_p", bufs=1))
        psum_t = ctx.enter_context(tc.psum_pool(name="psum_t", bufs=2))
        psum_s = ctx.enter_context(tc.psum_pool(name="psum_s", bufs=1))

        xs = keep.tile([P, PASSES * T], F32)
        nc.sync.dma_start(
            out=xs[:].rearrange("p (g t) -> p g t", t=T),
            in_=x_scale.rearrange("o (g p t) h w -> p g (o t h w)", p=P, t=T),
        )
        x_view = x_bytes.rearrange("b (g p t) h w -> b g p t (h w)", p=P, t=T)
        raw = {}

        def load_x(b, g, split):
            raw[b, g] = keep.tile([P, T, PIXELS], U8, name="raw_%d_%d" % (b, g), align_bytes=64)
            if split:
                for h in range(HALVES):
                    cols = slice(h * HALF, (h + 1) * HALF)
                    nc.sync.dma_start(out=raw[b, g][:, :, cols], in_=x_view[b, g][:, :, cols])
            else:
                nc.sync.dma_start(out=raw[b, g][:], in_=x_view[b, g])

        load_x(0, 0, True)
        load_x(0, 1, False)
        load_x(0, 2, False)

        bias_in = keep.tile([P, T], BF16)
        nc.sync.dma_start(out=bias_in[:], in_=bs1.rearrange("(p t) -> p t", t=T))
        s1_in = keep.tile([P, HIDDEN], U8, align_bytes=64)
        s2 = keep.tile([P, CLUSTERS], U8, align_bytes=64)
        nc.vector.memset(s1_in[:].bitcast(I32), 0)
        nc.vector.memset(s2[:].bitcast(I32), 0)
        for q in range(4):
            nc.sync.dma_start(
                out=s1_in[32 * q : 32 * q + 12, :].bitcast(I32),
                in_=Ws1_scales[:, 4 * q : 4 * q + 4, :].bitcast(I32),
            )
        for r in range(4):
            nc.sync.dma_start(
                out=s2[r:P:32, :].bitcast(I32),
                in_=Ws2_scales[0, r:16:4, :].bitcast(I32),
            )
        w1_in = []
        for g in range(PASSES):
            w = keep.tile([P, HIDDEN], I32, name="w1_in_%d" % g, align_bytes=64)
            nc.sync.dma_start(out=w[:], in_=Ws1_words[g].rearrange("p n t -> p (n t)").bitcast(I32))
            w1_in.append(w)
        w2 = keep.tile([P, CLUSTERS], I32, align_bytes=64)
        nc.sync.dma_start(out=w2[:], in_=Ws2_words[0].rearrange("p n t -> p (n t)").bitcast(I32))
        for b in range(1, IMAGES):
            for g in range(PASSES):
                load_x(b, g, False)

        ident = keep.tile([P, P], BF16)
        make_identity(nc, ident[:])
        ones = keep.tile([P, P], BF16)
        nc.gpsimd.memset(ones[:], 1.0 / P)
        mean_ones = keep.tile([P, P], BF16)
        nc.gpsimd.memset(mean_ones[:], 1.0 / PIXELS)
        one = keep.tile([P, 1], BF16)
        nc.gpsimd.memset(one[:], 1.0)
        first = keep.tile([P, 1], F32)
        nc.vector.memset(first[:], 1.0)
        warm = keep.tile([P, 1], F32)
        nc.scalar.activation(out=warm[:], in_=first[:], func=ACT.Exp)

        w1 = keep.tile([P, PASSES, HIDDEN], I32, align_bytes=64)
        s1 = keep.tile([P, HIDDEN], U8, align_bytes=64)

        bias = keep.tile([P, T], F32)

        def permute_weights():
            nc.vector.tensor_copy(out=bias[:], in_=bias_in[:])
            nc.vector.tensor_copy(
                out=s1[:].rearrange("p (t m) -> p m t", t=T), in_=s1_in[:].rearrange("p (m t) -> p m t", t=T)
            )
            for g in range(PASSES):
                nc.vector.tensor_copy(
                    out=w1[:, g, :].rearrange("p (t m) -> p t m", t=T),
                    in_=w1_in[g][:].rearrange("p (m t) -> p t m", t=T),
                )

        planes = {}
        mixed = {}
        xq = {}

        def widen(b, g, t, cols, vector):
            if (b, g) not in planes:
                planes[b, g] = work.tile([P, T, PIXELS], BF16, name="planes", bufs=6, align_bytes=64)
            plane = planes[b, g][:, t, cols]
            codes = raw[b, g][:, t, cols].bitcast(F8)
            factor = xs[:, g * T + t : g * T + t + 1]
            if vector:
                nc.vector.tensor_scalar(out=plane, in0=codes, scalar1=factor, scalar2=None, op0=ALU.mult)
            else:
                nc.scalar.activation(out=plane, in_=codes, func=ACT.Copy, scale=factor)

        def mix_x(k, g):
            b, start, width = steps[k]
            mixed[k, g] = work.tile([P, width * T], BF16, name="mixed", bufs=4, align_bytes=64)
            nc.vector.tensor_copy(
                out=mixed[k, g][:].rearrange("p (n t) -> p n t", t=T),
                in_=planes[b, g][:, :, start : start + width].rearrange("p t n -> p n t"),
            )

        def quantize_x(k, g):
            width = steps[k][2]
            codes = work.tile([P, width], U32, name="xcodes", bufs=8, align_bytes=64)
            scales = work.tile([P, width], U8, name="xscales", bufs=8, align_bytes=64)
            nc.vector.quantize_mx(out=codes[:].bitcast(F8X4), scales=scales[:], in_=mixed[k, g][:])
            xq[k, g] = (codes, scales)

        hidden = {}
        tops = {}
        sums = {}
        score = {}

        def hidden_tile(k, t):
            width = steps[k][2]
            if t == 0:
                hidden[k] = work.tile([P, T, width], BF16, name="hidden", bufs=2, align_bytes=64)
            acc = psum_acc.tile([P, width], F32, name="acc")
            for g in range(PASSES):
                codes, scales = xq[k, g]
                nc.tensor.matmul_mx(
                    out=acc[:],
                    lhsT=w1[:, g, t * P : (t + 1) * P].bitcast(F8X4),
                    lhsT_scale=s1[4 * g : P, t * P : (t + 1) * P],
                    rhs=codes[:].bitcast(F8X4),
                    rhs_scale=scales[:],
                    start=(g == 0),
                    stop=(g == PASSES - 1),
                )
            sums[k, t] = acc

        def relu_tile(k, t):
            nc.scalar.activation(out=hidden[k][:, t, :], in_=sums[k, t][:], func=ACT.Relu, bias=bias[:, t : t + 1])

        def mix_hidden(k):
            mixed[k, "h"] = work.tile([P, steps[k][2] * T], BF16, name="mixed", bufs=4, align_bytes=64)
            nc.vector.tensor_copy(
                out=mixed[k, "h"][:].rearrange("p (n t) -> p n t", t=T), in_=hidden[k][:].rearrange("p t n -> p n t")
            )

        def score_part(k):
            b, start, width = steps[k]
            codes = work.tile([P, width], U32, name="hcodes", bufs=2, align_bytes=64)
            scales = work.tile([P, width], U8, name="hscales", bufs=2, align_bytes=64)
            nc.vector.quantize_mx(out=codes[:].bitcast(F8X4), scales=scales[:], in_=mixed[k, "h"][:])
            h, offset = divmod(start, HALF)
            if offset == 0:
                score[b, h] = psum_p.tile([P, HALF], F32, name="score_%d" % h)
            part = score[b, h][:, offset : offset + width]
            nc.tensor.matmul_mx(
                out=part,
                lhsT=w2[:].bitcast(F8X4),
                lhsT_scale=s2[:],
                rhs=codes[:].bitcast(F8X4),
                rhs_scale=scales[:],
                start=True,
                stop=True,
            )
            if start == 0:
                tops[b] = [work.tile([P, 4], F32, name="tops"), 0]
            tile, n = tops[b]
            nc.vector.tensor_reduce(out=tile[:, n : n + 1], in_=part, axis=AX.X, op=ALU.max)
            tops[b][1] += 1

        def sinkhorn(b):
            st = {}

            def exps():
                neg_top = work.tile([P, 1], F32, name="neg_top")
                tile, n = tops[b]
                nc.vector.tensor_reduce(out=neg_top[:], in_=tile[:, 0:n], axis=AX.X, op=ALU.max, negate=True)
                st["e"] = work.tile([P, PIXELS], F32, name="e")
                st["sums"] = work.tile([P, HALVES], F32, name="sums")
                for h in range(HALVES):
                    nc.scalar.activation(
                        out=st["e"][:, h * HALF : (h + 1) * HALF],
                        in_=score[b, h][:],
                        func=ACT.Exp,
                        bias=neg_top[:],
                        accum_out=st["sums"][:, h : h + 1],
                    )

            def reciprocals(source, width, name):
                full = work.tile([P, width], F32, name=name + "_full", bufs=6)
                high = work.tile([P, width], BF16, name=name + "_high", bufs=6)
                nc.vector.reciprocal(out=full[:], in_=source)
                with nc.allow_low_precision(reason="the high part of a split; the low part follows"):
                    nc.vector.reciprocal(out=high[:], in_=source)
                st[name] = (full, high)

            def low_part(name, width):
                full, high = st[name]
                low = work.tile([P, width], BF16, name=name + "_low", bufs=6)
                nc.vector.tensor_tensor(out=low[:], in0=full[:], in1=high[:], op=ALU.subtract)
                st[name] = (full, high, low)

            def split_half(h):
                cols = slice(h * HALF, (h + 1) * HALF)
                nc.vector.tensor_copy(out=st["eh"][:, cols], in_=st["e"][:, cols])
                nc.vector.tensor_tensor(
                    out=st["el"][:, cols], in0=st["e"][:, cols], in1=st["eh"][:, cols], op=ALU.subtract
                )

            def first_rows():
                pool = psum_acc if b == IMAGES - 1 else psum_s
                st["small"] = pool.tile([P, 2 + CHUNKS], F32, name="acc" if b == IMAGES - 1 else "small")
                st["eh"] = work.tile([P, PIXELS], BF16, name="eh")
                st["el"] = work.tile([P, PIXELS], BF16, name="el")
                split_half(0)
                total = work.tile([P, 1], F32, name="total")
                nc.vector.tensor_tensor(out=total[:], in0=st["sums"][:, 0:1], in1=st["sums"][:, 1:2], op=ALU.add)
                reciprocals(total[:], 1, "w")
                st["dust"] = (one[:],)

            def split_e():
                split_half(1)
                low_part("w", 1)

            def turn():
                for part in ("eh", "el"):
                    st["turned", part] = psum_t.tile([P, CHUNKS, P], BF16, name="turned")
                    for j in range(CHUNKS):
                        nc.tensor.transpose(st["turned", part][:, j, :], st[part][:, j * P : (j + 1) * P], ident[:])

            def keep_turned():
                st["et"] = []
                for part in ("eh", "el"):
                    et = work.tile([P, CHUNKS, CLUSTERS], BF16, name="t" + part)
                    if b == IMAGES - 1 and part == "el":
                        nc.vector.tensor_copy(out=et[:], in_=st["turned", part][:])
                    else:
                        nc.scalar.copy(out=et[:], in_=st["turned", part][:])
                    st["et"].append(et)

            def column_sums():
                cols = st["small"][:, 2 : 2 + CHUNKS]
                for i, d in enumerate(st["dust"]):
                    nc.tensor.matmul(cols, lhsT=ones[:], rhs=d.to_broadcast([P, CHUNKS]), start=(i == 0), stop=False)
                full, high, low = st["w"]
                terms = [("eh", high), ("eh", low), ("el", high)]
                for i, (part, w) in enumerate(terms):
                    for j in range(CHUNKS):
                        nc.tensor.matmul(
                            cols[:, j : j + 1],
                            lhsT=st[part][:, j * P : (j + 1) * P],
                            rhs=w[:, 0:1],
                            start=False,
                            stop=(i == 2 and j == CHUNKS - 1),
                        )

            def columns():
                reciprocals(st["small"][:, 2 : 2 + CHUNKS], CHUNKS, "inv")

            def row_sums():
                low_part("inv", CHUNKS)
                full, high, low = st["inv"]
                th, tl = st["et"]
                terms = [(th, high), (th, low), (tl, high)]
                for i, (et, inv) in enumerate(terms):
                    for j in range(CHUNKS):
                        nc.tensor.matmul(
                            st["small"][:, 0:1],
                            lhsT=et[:, j, :],
                            rhs=inv[:, j : j + 1],
                            start=(i == 0 and j == 0),
                            stop=(i == 2 and j == CHUNKS - 1),
                        )
                for i, inv in enumerate((high, low)):
                    for j in range(CHUNKS):
                        nc.tensor.matmul(
                            st["small"][:, 1:2],
                            lhsT=mean_ones[:],
                            rhs=inv[:, j : j + 1],
                            start=(i == 0 and j == 0),
                            stop=(i == 1 and j == CHUNKS - 1),
                        )

            def rows():
                reciprocals(st["small"][:, 0:2], 2, "w")

            def row_parts():
                low_part("w", 2)
                full, high, low = st["w"]
                st["dust"] = (high[:, 1:2], low[:, 1:2])
                column_sums()

            def spread():
                low_part("inv", CHUNKS)
                full, high, low = st["inv"]
                for h in range(HALVES):
                    st["spread", h] = psum_t.tile([P, HALF], F32, name="turned")
                    for j in range(4):
                        c = 4 * h + j
                        for i, inv in enumerate((high, low)):
                            nc.tensor.matmul(
                                st["spread", h][:, j * P : (j + 1) * P],
                                lhsT=inv[:, c : c + 1].to_broadcast([P, P]),
                                rhs=ident[:],
                                start=(i == 0),
                                stop=(i == 1),
                            )

            def finish():
                for h in range(HALVES):
                    cols = slice(h * HALF, (h + 1) * HALF)
                    result = work.tile([P, HALF], F32, name="result")
                    nc.vector.scalar_tensor_tensor(
                        out=result[:],
                        in0=st["e"][:, cols],
                        scalar=st["w"][0][:, 0:1],
                        in1=st["spread", h][:],
                        op0=ALU.mult,
                        op1=ALU.mult,
                    )
                    nc.sync.dma_start(out=out[b][:, cols], in_=result[:])

            stages = [exps, None, None, first_rows, lambda: (split_e(), column_sums(), turn())]
            stages += [lambda: (keep_turned(), columns()), row_sums, rows, row_parts]
            for r in range(ROUNDS - 2):
                stages += [columns, row_sums, rows, row_parts]
            return stages + [columns, spread, finish]

        chains = {}

        def chain_step(b):
            if chains.get(b):
                part = chains[b].pop(0)
                if part is not None:
                    part()

        steps = [(b, h * HALF, HALF) for b in range(IMAGES) for h in range(HALVES)]
        steps[-1:] = [(IMAGES - 1, HALF, HALF // 2), (IMAGES - 1, HALF + HALF // 2, HALF // 2)]
        last = len(steps)
        scalar_queue = []
        vector_widen = {}
        for k, (b, start, width) in enumerate(steps):
            if b > 0 and start > 0:
                continue
            cols = slice(start, start + width) if b == 0 else slice(0, PIXELS)
            for g in range(PASSES):
                if k == 0:
                    on_vector = (2, 3)
                elif b > 0 and g == PASSES - 1:
                    on_vector = ()
                else:
                    on_vector = ()
                vector_widen[k, g] = [(b, g, t, cols) for t in on_vector]
                scalar_queue.extend([(b, g, t, cols) for t in range(T) if t not in on_vector])

        def widen_scalar(n):
            for i in range(n):
                if scalar_queue:
                    widen(*scalar_queue.pop(0), False)

        def widen_due(k, g):
            b, start, width = steps[k]
            while any(i[:2] == (b, g) and i[3].start <= start for i in scalar_queue):
                widen_scalar(1)

        def widen_vector(k, g):
            widen_due(k, g)
            for item in vector_widen.get((k, g), []):
                widen(*item, True)

        def schedule():
            widen_scalar(6)
            for k in range(last + 2):
                has_x = k < last
                has_hidden = 0 < k <= last
                unit = 2 if k == 0 else 1
                if has_hidden:
                    hidden_tile(k - 1, 0)
                    hidden_tile(k - 1, 1)
                if has_x:
                    widen_vector(k, 0)
                    mix_x(k, 0)
                widen_scalar(unit)
                if has_hidden:
                    relu_tile(k - 1, 0)
                chain_step(now[0])
                if k > 1:
                    score_part(k - 2)
                chain_step(now[0])
                if has_hidden:
                    hidden_tile(k - 1, 2)
                    hidden_tile(k - 1, 3)
                if has_x:
                    widen_vector(k, 1)
                    mix_x(k, 1)
                widen_scalar(unit)
                if has_hidden:
                    relu_tile(k - 1, 1)
                    relu_tile(k - 1, 2)
                chain_step(now[0])
                if has_x:
                    quantize_x(k, 0)
                if k > 1 and (k == last + 1 or steps[k - 2][0] < steps[k - 1][0]):
                    b = steps[k - 2][0]
                    chains[b] = sinkhorn(b)
                    now[0] = b
                    if b == IMAGES - 1:
                        chain_step(b)
                        now[0] = None
                chain_step(now[0])
                widen_scalar(unit)
                if has_hidden:
                    relu_tile(k - 1, 3)
                if has_x:
                    widen_vector(k, 2)
                    mix_x(k, 2)
                chain_step(now[0])
                if has_x:
                    quantize_x(k, 1)
                widen_scalar(unit)
                chain_step(now[0])
                if k == 0:
                    permute_weights()
                if has_hidden:
                    mix_hidden(k - 1)
                widen_scalar(unit)
                chain_step(now[0])
                if has_x:
                    quantize_x(k, 2)
                widen_scalar(unit)
                chain_step(now[0])
            for i in range(32):
                for b in reversed(range(IMAGES)):
                    chain_step(b)

        now = [None]
        schedule()
